import numpy as np
import ml_dtypes


def mxq(x, axis, fmt="e4m3"):
    dtype, down = {"e4m3": (ml_dtypes.float8_e4m3fn, 7), "e5m2": (ml_dtypes.float8_e5m2, 14)}[fmt]
    v = np.moveaxis(np.asarray(x, np.float32).astype(ml_dtypes.bfloat16).astype(np.float64), axis, -1)
    blocks = v.reshape(v.shape[:-1] + (-1, 32))
    amax = np.abs(blocks).max(-1, keepdims=True)
    byte = np.maximum(np.where(amax > 0, np.frexp(amax)[1] - 1 + 127, 0) - down, 1)
    scale = np.exp2(byte - 127.0)
    codes = (blocks / scale).astype(np.float32).astype(dtype).astype(np.float64)
    return np.moveaxis((codes * scale).reshape(v.shape), -1, axis)


WIDE = False


def mx_kscale(k):
    if not WIDE:
        return np.ones(k)
    levels = np.array([10, -10, 5, -5, 0])
    if k % 512:
        return np.exp2(np.random.permutation(np.resize(levels, k // 32))).repeat(32)
    a = np.empty((k // 512, 16))
    for p in range(k // 512):
        a[p, :8] = np.random.permutation(np.resize(levels, 8))
        for g in range(8):
            far = levels[np.abs(levels - a[p, g]) >= 10]
            a[p, g + 8] = far[np.random.randint(len(far))]
    return np.exp2(a.ravel()).repeat(32)


BF16 = ml_dtypes.bfloat16


def bf(x):
    return np.asarray(x, np.float32).astype(BF16)


def f64(x):
    return np.asarray(x).astype(np.float64)


B, G, DB, DR = 128, 16, 1024, 2048
T = B * G


def sigmoid(v):
    return 1.0 / (1.0 + np.exp(-v))


def mish(v):
    return v * np.tanh(np.log(1.0 + np.exp(v)))


def dmish(v):
    th = np.tanh(np.log(1.0 + np.exp(v)))
    return th + v * (1.0 - th * th) * sigmoid(v)


def setup_inputs():
    s = np.asarray(mx_kscale(T)).reshape(B, G, 1)
    u = np.asarray(mx_kscale(DB))
    x0 = bf(np.random.standard_normal((B, G, DB)))
    rf = bf(np.random.standard_normal((B, DR)))
    w0 = bf(np.random.standard_normal((DB, DB)) / np.sqrt(DB))
    b_bb = bf(np.random.standard_normal(DB) * 0.5)
    w_rf = bf(np.random.standard_normal((DB, DR)) / np.sqrt(DR))
    b_rf = bf(np.random.standard_normal(DB) * 0.5)
    g = bf(np.random.standard_normal((B, G, DB)) * np.exp2(np.random.randint(-6, 1, (B, G, 1))) * 4.0 / s * u)
    z = f64(x0) @ f64(w0).T + f64(b_bb)
    return {"BB_feature": bf(f64(x0) * s),
            "RF_feature": rf,
            "W_bbbb": bf(f64(w0) / u[:, None]),
            "b_bbbb": b_bb,
            "W_rfbb": w_rf,
            "b_rfbb": b_rf,
            "z": np.asarray(z, np.float32),
            "grad_out": g}


def reference(BB_feature, RF_feature, W_bbbb, b_bbbb, W_rfbb, b_rfbb, z, grad_out):
    dz = (f64(grad_out) * dmish(f64(z))).reshape(T, DB)
    x2 = f64(BB_feature).reshape(T, DB)
    dx = mxq(dz, 1, "e5m2") @ mxq(f64(W_bbbb), 0, "e4m3")
    dw = mxq(dz, 0, "e5m2").T @ mxq(x2, 0, "e4m3")
    return dx.reshape(B, G, DB), dw

@@ -1,0 +1,306 @@
+from contextlib import ExitStack
+
+import concourse.mybir as mybir
+from concourse.masks import make_identity
+
+T, D = 2048, 1024
+FLOPS = 2 * 2 * T * D * D
+BYTES = T * D * (2 + 4 + 2 + 4) + D * D * (2 + 4)
+
+F32 = mybir.dt.float32
+BF16 = mybir.dt.bfloat16
+U32 = mybir.dt.uint32
+U8 = mybir.dt.uint8
+E4 = mybir.dt.float8_e4m3fn_x4
+E5 = mybir.dt.float8_e5m2_x4
+ACT = mybir.ActivationFunctionType
+ALU = mybir.AluOpType
+
+P = 128
+NB = 8
+
+
+def tile_gnn_layer_pb_v_kernel(
+    tc, BB_feature, RF_feature, W_bbbb, b_bbbb, W_rfbb, b_rfbb, z, grad_out, out_0, out_1
+):
+    nc = tc.nc
+    x_v = BB_feature.flatten_outer_dims().rearrange("(c p j) w -> p c j w", p=P, j=4)
+    z_v = z.flatten_outer_dims().rearrange("(c p j) w -> p c j w", p=P, j=4)
+    g_v = grad_out.flatten_outer_dims().rearrange("(c p j) w -> p c j w", p=P, j=4)
+    o0_v = out_0.flatten_outer_dims().rearrange("(c p j) w -> p c j w", p=P, j=4)
+    w_v = W_bbbb.rearrange("(c p j) w -> p c j w", p=P, j=4)
+
+    with ExitStack() as ctx:
+        keep = ctx.enter_context(tc.tile_pool(name="keep", bufs=1))
+        work = ctx.enter_context(tc.tile_pool(name="work", bufs=2))
+        psum = ctx.enter_context(tc.psum_pool(name="psum", bufs=2))
+
+        ident = keep.tile([P, P], F32, name="ident")
+        make_identity(nc, ident[:])
+        identb = keep.tile([P, P], BF16, name="identb")
+        make_identity(nc, identb[:])
+        warm = keep.tile([P, 8], F32, name="warm")
+        nc.vector.memset(warm[:], 0.0)
+
+        w_codes = keep.tile([P, 2, D], U32, name="w_codes", align_bytes=64)
+        w_scales = keep.tile([P, 2, D], U8, name="w_scales", align_bytes=64)
+        x_codes = keep.tile([P, 4, D], U32, name="x_codes", align_bytes=64)
+        x_scales = keep.tile([P, 4, D], U8, name="x_scales", align_bytes=64)
+        d_codes = keep.tile([P, 4, D], U32, name="d_codes", align_bytes=64)
+        d_scales = keep.tile([P, 4, D], U8, name="d_scales", align_bytes=64)
+
+        ctx.enter_context(tc.manual_schedule())
+        nc.scalar.activation(out=warm[:, 4:5], in_=warm[:, 0:1], func=ACT.Sigmoid)
+
+        zt, st, ut, gt, dzp, dzg, gtr, tq, ts, raw = {}, {}, {}, {}, {}, {}, {}, {}, {}, {}
+
+        def cols(h):
+            return slice(512 * h, 512 * (h + 1))
+
+        def load_z(k):
+            zt[k] = work.tile([P, 2048], F32, name="zt", bufs=4)
+            nc.sync.dma_start(out=zt[k][:].rearrange("p (j w) -> p j w", j=4), in_=z_v[:, k // 2, :, cols(k % 2)])
+
+        def load_g(k):
+            gt[k] = work.tile([P, 2048], BF16, name="gt", bufs=4)
+            nc.sync.dma_start(out=gt[k][:].rearrange("p (j w) -> p j w", j=4), in_=g_v[:, k // 2, :, cols(k % 2)])
+
+        def load_raw(key, src, split=False):
+            raw[key] = work.tile([P, 4, D], BF16, name="raw", bufs=2)
+            if split:
+                for ih in range(2):
+                    nc.sync.dma_start(out=raw[key][:, :, cols(ih)], in_=src[:, :, cols(ih)])
+            else:
+                nc.sync.dma_start(out=raw[key][:], in_=src)
+
+        def s1(k):
+            st[k] = work.tile([P, 2048], F32, name="st", bufs=3)
+            nc.scalar.activation(out=st[k][:], in_=zt[k][:], func=ACT.Sigmoid)
+
+        def s2(k):
+            ut[k] = work.tile([P, 2048], F32, name="ut", bufs=4)
+            nc.scalar.activation(out=ut[k][:], in_=st[k][:], func=ACT.Ln, bias=1.0, scale=-1.0)
+
+        def s3(k):
+            nc.scalar.activation(out=ut[k][:], in_=ut[k][:], func=ACT.Sigmoid, scale=-2.0)
+
+        def v1(k):
+            nc.vector.scalar_tensor_tensor(out=zt[k][:], in0=zt[k][:], scalar=-4.0, in1=st[k][:], op0=ALU.mult, op1=ALU.mult)
+
+        def v2(k):
+            nc.vector.scalar_tensor_tensor(out=zt[k][:], in0=ut[k][:], scalar=1.0, in1=zt[k][:], op0=ALU.subtract, op1=ALU.mult)
+
+        def v3(k):
+            nc.vector.scalar_tensor_tensor(out=zt[k][:], in0=zt[k][:], scalar=2.0, in1=ut[k][:], op0=ALU.add, op1=ALU.mult)
+
+        def v4(k):
+            dzp[k] = work.tile([P, 2048], BF16, name="dzp", bufs=3, align_bytes=64)
+            nc.vector.scalar_tensor_tensor(out=dzp[k][:], in0=zt[k][:], scalar=1.0, in1=gt[k][:], op0=ALU.subtract, op1=ALU.mult)
+
+        def interleave(copy, dst, src):
+            copy(out=dst.rearrange("p (w j) -> p w j", j=4), in_=src.rearrange("p j w -> p w j"))
+
+        def il_direct(k, copy):
+            dzg[k] = work.tile([P, 2048], BF16, name="dzg", bufs=2, align_bytes=64)
+            interleave(copy, dzg[k][:], dzp[k][:].rearrange("p (j w) -> p j w", j=4))
+
+        def il(k, copies):
+            dzg[k] = work.tile([P, 2048], BF16, name="dzg", bufs=2, align_bytes=64)
+            src = dzp[k][:].rearrange("p (j w) -> p w j", j=4)
+            for half in range(2):
+                ilp = psum.tile([P, 1024], BF16, name="ilp", tag="bank", bufs=8)
+                for qd in range(2):
+                    w0 = 256 * half + 128 * qd
+                    nc.tensor.matmul(
+                        out=ilp[:, 512 * qd : 512 * (qd + 1)].rearrange("p (w j) -> p w j", j=4),
+                        lhsT=identb[:],
+                        rhs=src[:, w0 : w0 + 128, :],
+                        start=True,
+                        stop=True,
+                    )
+                copies[half](out=dzg[k][:, 1024 * half : 1024 * (half + 1)], in_=ilp[:])
+
+        def q1(k):
+            nc.vector.quantize_mx(out=d_codes[:, k // 2, cols(k % 2)].bitcast(E5), scales=d_scales[:, k // 2, cols(k % 2)], in_=dzg[k][:])
+
+        def tp(k, copies):
+            gtr[k] = work.tile([P, 2048], BF16, name="gtr", bufs=2, align_bytes=64)
+            words = dzp[k][:].bitcast(F32)
+            dst = gtr[k][:].bitcast(F32).rearrange("p (j r u) -> p j r u", j=4, u=2)
+            for half in range(2):
+                xt = psum.tile([P, 4, P], F32, name="xt", tag="bank", bufs=8)
+                for jj in range(2):
+                    j = 2 * half + jj
+                    for u in range(2):
+                        nc.tensor.transpose(xt[:, 2 * jj + u, :], words[:, 256 * j + u : 256 * (j + 1) : 2], ident[:])
+                copies[half](out=dst[:, 2 * half : 2 * half + 2], in_=xt[:].rearrange("p (j u) r -> p j r u", u=2))
+
+        def q2(k):
+            tq[k] = work.tile([P, 512], U32, name="tq", bufs=4, align_bytes=64)
+            ts[k] = work.tile([P, 512], U8, name="ts", bufs=4, align_bytes=64)
+            nc.vector.quantize_mx(out=tq[k][:].bitcast(E5), scales=ts[k][:], in_=gtr[k][:])
+
+        grp = {}
+
+        def prep_il(key, ih, copy):
+            grp[(key, ih)] = work.tile([P, 2048], BF16, name="grp", bufs=2, align_bytes=64)
+            interleave(copy, grp[(key, ih)][:], raw[key][:, :, cols(ih)])
+
+        def prep_q(key, ih, codes, scales):
+            nc.vector.quantize_mx(out=codes[:, cols(ih)].bitcast(E4), scales=scales[:, cols(ih)], in_=grp[(key, ih)][:])
+
+        def mm0(c, j, copies):
+            o_sb = work.tile([P, D], F32, name="o_sb", bufs=4)
+            for ih in range(2):
+                acc = psum.tile([P, 512], F32, name="acc", tag="bank", bufs=8)
+                for h in range(2):
+                    k = 2 * c + h
+                    nc.tensor.matmul_mx(
+                        out=acc[:],
+                        lhsT=tq[k][:, P * j : P * (j + 1)].bitcast(E5),
+                        lhsT_scale=ts[k][:, P * j : P * (j + 1)],
+                        rhs=w_codes[:, h, cols(ih)].bitcast(E4),
+                        rhs_scale=w_scales[:, h, cols(ih)],
+                        start=(h == 0),
+                        stop=(h == 1),
+                    )
+                copies[ih](out=o_sb[:, cols(ih)], in_=acc[:])
+            nc.sync.dma_start(out=o0_v[:, c, j, :], in_=o_sb[:])
+
+        def passes1(acc, a, ih, cs):
+            for c in cs:
+                nc.tensor.matmul_mx(
+                    out=acc[:],
+                    lhsT=d_codes[:, c, P * a : P * (a + 1)].bitcast(E5),
+                    lhsT_scale=d_scales[:, c, P * a : P * (a + 1)],
+                    rhs=x_codes[:, c, cols(ih)].bitcast(E4),
+                    rhs_scale=x_scales[:, c, cols(ih)],
+                    start=(c == cs[0]),
+                    stop=(c == cs[-1]),
+                )
+
+        def mm1(a, copies):
+            o_sb = work.tile([P, D], F32, name="o_sb", bufs=4)
+            for ih in range(2):
+                acc = psum.tile([P, 512], F32, name="acc", tag="bank", bufs=8)
+                passes1(acc, a, ih, (0, 1, 2, 3))
+                copies[ih](out=o_sb[:, cols(ih)], in_=acc[:])
+            nc.sync.dma_start(out=out_1[P * a : P * (a + 1), :], in_=o_sb[:])
+
+        part = {}
+
+        def mm1_early(a, copies):
+            if a % 2 == 0:
+                part[a // 2] = work.tile([P, 2048], F32, name="st", bufs=3)
+            for ih in range(2):
+                acc = psum.tile([P, 512], F32, name="acc", tag="bank", bufs=8)
+                passes1(acc, a, ih, (0, 1, 2))
+                lo = 1024 * (a % 2) + 512 * ih
+                copies[ih](out=part[a // 2][:, lo : lo + 512], in_=acc[:])
+
+        def mm1_late(a):
+            for ih in range(2):
+                acc = psum.tile([P, 512], F32, name="acc", tag="bank", bufs=8)
+                passes1(acc, a, ih, (3,))
+                lo = 1024 * (a % 2) + 512 * ih
+                nc.vector.tensor_tensor(out=part[a // 2][:, lo : lo + 512], in0=acc[:], in1=part[a // 2][:, lo : lo + 512], op=ALU.add)
+            lo = 1024 * (a % 2)
+            nc.sync.dma_start(out=out_1[P * a : P * (a + 1), :], in_=part[a // 2][:, lo : lo + 1024])
+
+        VC = nc.vector.tensor_copy
+        SC = nc.scalar.copy
+
+        def prep(key, codes, scales):
+            prep_il(key, 0, VC)
+            prep_il(key, 1, VC)
+            prep_q(key, 0, codes, scales)
+            prep_q(key, 1, codes, scales)
+
+        O0 = {0: ((SC, VC), (SC, SC), (SC, VC), (SC, SC)), 1: ((SC, VC), (SC, SC), (SC, VC), (SC, SC)), 2: ((SC, VC), (SC, SC), (SC, VC), (SC, SC))}
+        XC = {0: (x_codes[:, 0], x_scales[:, 0]), 1: (x_codes[:, 1], x_scales[:, 1]), 2: (x_codes[:, 2], x_scales[:, 2]), 3: (x_codes[:, 3], x_scales[:, 3])}
+        load_raw("w0", w_v[:, 0], split=True)
+        load_z(0)
+        load_z(1)
+        load_raw("w1", w_v[:, 1], split=True)
+        load_g(0)
+        load_g(1)
+        prep("w0", w_codes[:, 0], w_scales[:, 0])
+        load_raw("x0", x_v[:, 0])
+        load_z(2)
+        load_z(3)
+        s1(0)
+        s1(1)
+        s2(0)
+        s2(1)
+        prep("w1", w_codes[:, 1], w_scales[:, 1])
+        load_raw("x1", x_v[:, 1])
+        load_g(2)
+        load_g(3)
+        v1(0)
+        v1(1)
+        s3(0)
+        s3(1)
+        prep("x0", XC[0][0], XC[0][1])
+        load_raw("x2", x_v[:, 2])
+
+        for c in range(3):
+            a, b = 2 * c, 2 * c + 1
+            v2(a)
+            v2(b)
+            v3(a)
+            v3(b)
+            v4(a)
+            v4(b)
+            s1(a + 2)
+            s1(b + 2)
+            s2(a + 2)
+            s2(b + 2)
+            if c < 2:
+                load_z(a + 4)
+                load_z(b + 4)
+                load_g(a + 4)
+                load_g(b + 4)
+            il(a, (SC, SC))
+            tp(a, (SC, SC))
+            il(b, (SC, SC))
+            tp(b, (SC, SC))
+            v1(a + 2)
+            v1(b + 2)
+            s3(a + 2)
+            s3(b + 2)
+            q1(a)
+            q2(a)
+            q1(b)
+            q2(b)
+            prep_il("x%d" % (c + 1), 0, VC)
+            prep_il("x%d" % (c + 1), 1, VC)
+            for j in range(4):
+                mm0(c, j, O0[c][j])
+            prep_q("x%d" % (c + 1), 0, XC[c + 1][0], XC[c + 1][1])
+            prep_q("x%d" % (c + 1), 1, XC[c + 1][0], XC[c + 1][1])
+            if c == 0:
+                load_raw("x3", x_v[:, 3])
+        v2(6)
+        v3(6)
+        v4(6)
+        for a in (4, 5, 6, 7):
+            mm1_early(a, (SC, SC))
+        il_direct(6, SC)
+        tp(6, (SC, SC))
+        v2(7)
+        q1(6)
+        v3(7)
+        q2(6)
+        v4(7)
+        for a in (0, 1):
+            mm1(a, (SC, SC))
+        il_direct(7, VC)
+        tp(7, (SC, SC))
+        q1(7)
+        q2(7)
+        mm1(2, (SC, SC))
+        for a in (4, 5, 6, 7):
+            mm1_late(a)
+        for j in range(4):
+            mm0(3, j, (SC, SC))
+        mm1(3, (SC, VC))

@@ -98,7 +98,7 @@ def tile_gnn_layer_pb_v_kernel(
             nc.vector.scalar_tensor_tensor(out=dzp[k][:], in0=zt[k][:], scalar=1.0, in1=gt[k][:], op0=ALU.subtract, op1=ALU.mult)
 
         def interleave(copy, dst, src):
-            copy(out=dst.rearrange("p (w j) -> p w j", j=4), in_=src.rearrange("p j w -> p w j"))
+            copy(out=dst.rearrange("p (c i j) -> p c j i", i=4, j=4), in_=src.rearrange("p j (c i) -> p c j i", i=4))
 
         def il_direct(k, copy):
             dzg[k] = work.tile([P, 2048], BF16, name="dzg", bufs=2, align_bytes=64)
@@ -216,32 +216,65 @@ def tile_gnn_layer_pb_v_kernel(
             prep_q(key, 0, codes, scales)
             prep_q(key, 1, codes, scales)
 
-        O0 = {0: ((SC, VC), (SC, SC), (SC, VC), (SC, SC)), 1: ((SC, VC), (SC, SC), (SC, VC), (SC, SC)), 2: ((SC, VC), (SC, SC), (SC, VC), (SC, SC))}
+
+        def mm1_open(a_list):
+            accs = {}
+            for a in a_list:
+                for ih in range(2):
+                    accs[(a, ih)] = psum.tile([P, 512], F32, name="acc", tag="bank", bufs=8)
+                    for c in (0, 1, 2):
+                        nc.tensor.matmul_mx(
+                            out=accs[(a, ih)][:],
+                            lhsT=d_codes[:, c, P * a : P * (a + 1)].bitcast(E5),
+                            lhsT_scale=d_scales[:, c, P * a : P * (a + 1)],
+                            rhs=x_codes[:, c, cols(ih)].bitcast(E4),
+                            rhs_scale=x_scales[:, c, cols(ih)],
+                            start=(c == 0),
+                            stop=False,
+                        )
+            return accs
+
+        def mm1_close(accs, a_list, copies):
+            for a in a_list:
+                o_sb = work.tile([P, D], F32, name="o_sb", bufs=4)
+                for ih in range(2):
+                    nc.tensor.matmul_mx(
+                        out=accs[(a, ih)][:],
+                        lhsT=d_codes[:, 3, P * a : P * (a + 1)].bitcast(E5),
+                        lhsT_scale=d_scales[:, 3, P * a : P * (a + 1)],
+                        rhs=x_codes[:, 3, cols(ih)].bitcast(E4),
+                        rhs_scale=x_scales[:, 3, cols(ih)],
+                        start=False,
+                        stop=True,
+                    )
+                    copies[ih](out=o_sb[:, cols(ih)], in_=accs[(a, ih)][:])
+                nc.sync.dma_start(out=out_1[P * a : P * (a + 1), :], in_=o_sb[:])
+        O0 = {0: ((SC, VC), (SC, SC), (SC, SC), (SC, SC)), 1: ((SC, VC), (SC, SC), (SC, SC), (SC, SC)), 2: ((SC, VC), (SC, SC), (SC, SC), (SC, SC))}
         XC = {0: (x_codes[:, 0], x_scales[:, 0]), 1: (x_codes[:, 1], x_scales[:, 1]), 2: (x_codes[:, 2], x_scales[:, 2]), 3: (x_codes[:, 3], x_scales[:, 3])}
-        load_raw("w0", w_v[:, 0], split=True)
         load_z(0)
+        load_raw("w0", w_v[:, 0])
         load_z(1)
-        load_raw("w1", w_v[:, 1], split=True)
+        load_raw("w1", w_v[:, 1])
         load_g(0)
         load_g(1)
+        s1(0)
         prep("w0", w_codes[:, 0], w_scales[:, 0])
         load_raw("x0", x_v[:, 0])
         load_z(2)
         load_z(3)
-        s1(0)
         s1(1)
+        v1(0)
         s2(0)
         s2(1)
         prep("w1", w_codes[:, 1], w_scales[:, 1])
         load_raw("x1", x_v[:, 1])
         load_g(2)
         load_g(3)
-        v1(0)
         v1(1)
-        s3(0)
-        s3(1)
         prep("x0", XC[0][0], XC[0][1])
         load_raw("x2", x_v[:, 2])
+        s3(0)
+        s3(1)
 
         for c in range(3):
             a, b = 2 * c, 2 * c + 1
@@ -276,31 +309,34 @@ def tile_gnn_layer_pb_v_kernel(
             prep_il("x%d" % (c + 1), 1, VC)
             for j in range(4):
                 mm0(c, j, O0[c][j])
-            prep_q("x%d" % (c + 1), 0, XC[c + 1][0], XC[c + 1][1])
-            prep_q("x%d" % (c + 1), 1, XC[c + 1][0], XC[c + 1][1])
+            if c < 2:
+                prep_q("x%d" % (c + 1), 0, XC[c + 1][0], XC[c + 1][1])
+                prep_q("x%d" % (c + 1), 1, XC[c + 1][0], XC[c + 1][1])
             if c == 0:
                 load_raw("x3", x_v[:, 3])
         v2(6)
+        prep_q("x3", 0, XC[3][0], XC[3][1])
         v3(6)
+        prep_q("x3", 1, XC[3][0], XC[3][1])
         v4(6)
         for a in (4, 5, 6, 7):
             mm1_early(a, (SC, SC))
         il_direct(6, SC)
         tp(6, (SC, SC))
+        opened = mm1_open((0, 1))
         v2(7)
         q1(6)
         v3(7)
         q2(6)
         v4(7)
-        for a in (0, 1):
-            mm1(a, (SC, SC))
+        mm1_close(opened, (0, 1), (SC, SC))
+        mm1(2, (SC, SC))
         il_direct(7, VC)
         tp(7, (SC, SC))
         q1(7)
         q2(7)
-        mm1(2, (SC, SC))
+        mm1(3, (SC, SC))
         for a in (4, 5, 6, 7):
             mm1_late(a)
         for j in range(4):
             mm0(3, j, (SC, SC))
-        mm1(3, (SC, VC))

@@ -74,7 +74,7 @@ def tile_gnn_layer_pb_v_kernel(
                 nc.sync.dma_start(out=raw[key][:], in_=src)
 
         def s1(k):
-            st[k] = work.tile([P, 2048], F32, name="st", bufs=3)
+            st[k] = work.tile([P, 2048], F32, name="st", bufs=4)
             nc.scalar.activation(out=st[k][:], in_=zt[k][:], func=ACT.Sigmoid)
 
         def s2(k):
@@ -88,13 +88,13 @@ def tile_gnn_layer_pb_v_kernel(
             nc.vector.scalar_tensor_tensor(out=zt[k][:], in0=zt[k][:], scalar=-4.0, in1=st[k][:], op0=ALU.mult, op1=ALU.mult)
 
         def v2(k):
-            nc.vector.scalar_tensor_tensor(out=zt[k][:], in0=ut[k][:], scalar=1.0, in1=zt[k][:], op0=ALU.subtract, op1=ALU.mult)
+            nc.vector.scalar_tensor_tensor(out=st[k][:], in0=ut[k][:], scalar=1.0, in1=zt[k][:], op0=ALU.subtract, op1=ALU.mult)
 
         def v3(k):
-            nc.vector.scalar_tensor_tensor(out=zt[k][:], in0=zt[k][:], scalar=2.0, in1=ut[k][:], op0=ALU.add, op1=ALU.mult)
+            nc.vector.scalar_tensor_tensor(out=zt[k][:], in0=st[k][:], scalar=2.0, in1=ut[k][:], op0=ALU.add, op1=ALU.mult)
 
         def v4(k):
-            dzp[k] = work.tile([P, 2048], BF16, name="dzp", bufs=3, align_bytes=64)
+            dzp[k] = work.tile([P, 2048], BF16, name="dzp", bufs=2, align_bytes=64)
             nc.vector.scalar_tensor_tensor(out=dzp[k][:], in0=zt[k][:], scalar=1.0, in1=gt[k][:], op0=ALU.subtract, op1=ALU.mult)
 
         def interleave(copy, dst, src):
@@ -189,14 +189,19 @@ def tile_gnn_layer_pb_v_kernel(
 
         part = {}
 
-        def mm1_early(a, copies):
-            if a % 2 == 0:
-                part[a // 2] = work.tile([P, 2048], F32, name="st", bufs=3)
+        eacc = {}
+
+        def early_mm(a):
             for ih in range(2):
-                acc = psum.tile([P, 512], F32, name="acc", tag="bank", bufs=8)
-                passes1(acc, a, ih, (0, 1, 2))
+                eacc[(a, ih)] = psum.tile([P, 512], F32, name="acc", tag="bank", bufs=8)
+                passes1(eacc[(a, ih)], a, ih, (0, 1, 2))
+
+        def early_copy(a):
+            if a % 2 == 0:
+                part[a // 2] = work.tile([P, 2048], F32, name="st", bufs=4)
+            for ih in range(2):
                 lo = 1024 * (a % 2) + 512 * ih
-                copies[ih](out=part[a // 2][:, lo : lo + 512], in_=acc[:])
+                SC(out=part[a // 2][:, lo : lo + 512], in_=eacc[(a, ih)][:])
 
         def mm1_late(a):
             for ih in range(2):
@@ -319,10 +324,15 @@ def tile_gnn_layer_pb_v_kernel(
         v3(6)
         prep_q("x3", 1, XC[3][0], XC[3][1])
         v4(6)
-        for a in (4, 5, 6, 7):
-            mm1_early(a, (SC, SC))
+        for a in (4, 5):
+            early_mm(a)
+            early_copy(a)
+        for a in (6, 7):
+            early_mm(a)
         il_direct(6, SC)
         tp(6, (SC, SC))
+        for a in (6, 7):
+            early_copy(a)
         opened = mm1_open((0, 1))
         v2(7)
         q1(6)

@@ -74,7 +74,7 @@ def tile_gnn_layer_pb_v_kernel(
                 nc.sync.dma_start(out=raw[key][:], in_=src)
 
         def s1(k):
-            st[k] = work.tile([P, 2048], F32, name="st", bufs=4)
+            st[k] = work.tile([P, 2048], F32, name="st", bufs=3)
             nc.scalar.activation(out=st[k][:], in_=zt[k][:], func=ACT.Sigmoid)
 
         def s2(k):
@@ -88,13 +88,13 @@ def tile_gnn_layer_pb_v_kernel(
             nc.vector.scalar_tensor_tensor(out=zt[k][:], in0=zt[k][:], scalar=-4.0, in1=st[k][:], op0=ALU.mult, op1=ALU.mult)
 
         def v2(k):
-            nc.vector.scalar_tensor_tensor(out=st[k][:], in0=ut[k][:], scalar=1.0, in1=zt[k][:], op0=ALU.subtract, op1=ALU.mult)
+            nc.vector.scalar_tensor_tensor(out=zt[k][:], in0=ut[k][:], scalar=1.0, in1=zt[k][:], op0=ALU.subtract, op1=ALU.mult)
 
         def v3(k):
-            nc.vector.scalar_tensor_tensor(out=zt[k][:], in0=st[k][:], scalar=2.0, in1=ut[k][:], op0=ALU.add, op1=ALU.mult)
+            nc.vector.scalar_tensor_tensor(out=zt[k][:], in0=zt[k][:], scalar=2.0, in1=ut[k][:], op0=ALU.add, op1=ALU.mult)
 
         def v4(k):
-            dzp[k] = work.tile([P, 2048], BF16, name="dzp", bufs=2, align_bytes=64)
+            dzp[k] = work.tile([P, 2048], BF16, name="dzp", bufs=3, align_bytes=64)
             nc.vector.scalar_tensor_tensor(out=dzp[k][:], in0=zt[k][:], scalar=1.0, in1=gt[k][:], op0=ALU.subtract, op1=ALU.mult)
 
         def interleave(copy, dst, src):
@@ -198,7 +198,7 @@ def tile_gnn_layer_pb_v_kernel(
 
         def early_copy(a):
             if a % 2 == 0:
-                part[a // 2] = work.tile([P, 2048], F32, name="st", bufs=4)
+                part[a // 2] = work.tile([P, 2048], F32, name="st", bufs=3)
             for ih in range(2):
                 lo = 1024 * (a % 2) + 512 * ih
                 SC(out=part[a // 2][:, lo : lo + 512], in_=eacc[(a, ih)][:])
@@ -324,29 +324,22 @@ def tile_gnn_layer_pb_v_kernel(
         v3(6)
         prep_q("x3", 1, XC[3][0], XC[3][1])
         v4(6)
-        for a in (4, 5):
-            early_mm(a)
-            early_copy(a)
-        for a in (6, 7):
-            early_mm(a)
+        opened = mm1_open((0, 1, 2))
         il_direct(6, SC)
         tp(6, (SC, SC))
-        for a in (6, 7):
-            early_copy(a)
-        opened = mm1_open((0, 1))
         v2(7)
         q1(6)
         v3(7)
         q2(6)
         v4(7)
-        mm1_close(opened, (0, 1), (SC, SC))
-        mm1(2, (SC, SC))
+        mm1_close(opened, (0, 1, 2), (SC, SC))
+        mm1(3, (SC, SC))
+        opened2 = mm1_open((4, 5, 6))
         il_direct(7, VC)
         tp(7, (SC, SC))
         q1(7)
         q2(7)
-        mm1(3, (SC, SC))
-        for a in (4, 5, 6, 7):
-            mm1_late(a)
+        mm1_close(opened2, (4, 5, 6), (SC, VC))
+        mm1(7, (SC, VC))
         for j in range(4):
-            mm0(3, j, (SC, SC))
+            mm0(3, j, (SC, VC))

@@ -74,7 +74,7 @@ def tile_gnn_layer_pb_v_kernel(
                 nc.sync.dma_start(out=raw[key][:], in_=src)
 
         def s1(k):
-            st[k] = work.tile([P, 2048], F32, name="st", bufs=3)
+            st[k] = work.tile([P, 2048], F32, name="st", bufs=4)
             nc.scalar.activation(out=st[k][:], in_=zt[k][:], func=ACT.Sigmoid)
 
         def s2(k):
@@ -88,13 +88,13 @@ def tile_gnn_layer_pb_v_kernel(
             nc.vector.scalar_tensor_tensor(out=zt[k][:], in0=zt[k][:], scalar=-4.0, in1=st[k][:], op0=ALU.mult, op1=ALU.mult)
 
         def v2(k):
-            nc.vector.scalar_tensor_tensor(out=zt[k][:], in0=ut[k][:], scalar=1.0, in1=zt[k][:], op0=ALU.subtract, op1=ALU.mult)
+            nc.vector.scalar_tensor_tensor(out=st[k][:], in0=ut[k][:], scalar=1.0, in1=zt[k][:], op0=ALU.subtract, op1=ALU.mult)
 
         def v3(k):
-            nc.vector.scalar_tensor_tensor(out=zt[k][:], in0=zt[k][:], scalar=2.0, in1=ut[k][:], op0=ALU.add, op1=ALU.mult)
+            nc.vector.scalar_tensor_tensor(out=zt[k][:], in0=st[k][:], scalar=2.0, in1=ut[k][:], op0=ALU.add, op1=ALU.mult)
 
         def v4(k):
-            dzp[k] = work.tile([P, 2048], BF16, name="dzp", bufs=3, align_bytes=64)
+            dzp[k] = work.tile([P, 2048], BF16, name="dzp", bufs=2, align_bytes=64)
             nc.vector.scalar_tensor_tensor(out=dzp[k][:], in0=zt[k][:], scalar=1.0, in1=gt[k][:], op0=ALU.subtract, op1=ALU.mult)
 
         def interleave(copy, dst, src):
@@ -198,7 +198,7 @@ def tile_gnn_layer_pb_v_kernel(
 
         def early_copy(a):
             if a % 2 == 0:
-                part[a // 2] = work.tile([P, 2048], F32, name="st", bufs=3)
+                part[a // 2] = work.tile([P, 2048], F32, name="st", bufs=4)
             for ih in range(2):
                 lo = 1024 * (a % 2) + 512 * ih
                 SC(out=part[a // 2][:, lo : lo + 512], in_=eacc[(a, ih)][:])
@@ -254,7 +254,7 @@ def tile_gnn_layer_pb_v_kernel(
                     )
                     copies[ih](out=o_sb[:, cols(ih)], in_=accs[(a, ih)][:])
                 nc.sync.dma_start(out=out_1[P * a : P * (a + 1), :], in_=o_sb[:])
-        O0 = {0: ((SC, VC), (SC, SC), (SC, SC), (SC, SC)), 1: ((SC, VC), (SC, SC), (SC, SC), (SC, SC)), 2: ((SC, VC), (SC, SC), (SC, SC), (SC, SC))}
+        O0 = {0: ((SC, SC), (SC, SC), (SC, SC), (SC, SC)), 1: ((SC, SC), (SC, SC), (SC, SC), (SC, SC)), 2: ((SC, SC), (SC, SC), (SC, SC), (SC, SC))}
         XC = {0: (x_codes[:, 0], x_scales[:, 0]), 1: (x_codes[:, 1], x_scales[:, 1]), 2: (x_codes[:, 2], x_scales[:, 2]), 3: (x_codes[:, 3], x_scales[:, 3])}
         load_z(0)
         load_raw("w0", w_v[:, 0])
@@ -300,7 +300,7 @@ def tile_gnn_layer_pb_v_kernel(
                 load_g(b + 4)
             il(a, (SC, SC))
             tp(a, (SC, SC))
-            il(b, (SC, SC))
+            il_direct(b, VC)
             tp(b, (SC, SC))
             v1(a + 2)
             v1(b + 2)
@@ -324,22 +324,29 @@ def tile_gnn_layer_pb_v_kernel(
         v3(6)
         prep_q("x3", 1, XC[3][0], XC[3][1])
         v4(6)
-        opened = mm1_open((0, 1, 2))
+        for a in (4, 5):
+            early_mm(a)
+            early_copy(a)
+        for a in (6, 7):
+            early_mm(a)
         il_direct(6, SC)
         tp(6, (SC, SC))
+        for a in (6, 7):
+            early_copy(a)
+        opened = mm1_open((0, 1))
         v2(7)
         q1(6)
         v3(7)
         q2(6)
         v4(7)
-        mm1_close(opened, (0, 1, 2), (SC, SC))
-        mm1(3, (SC, SC))
-        opened2 = mm1_open((4, 5, 6))
+        mm1_close(opened, (0, 1), (SC, SC))
+        mm1(2, (SC, SC))
         il_direct(7, VC)
         tp(7, (SC, SC))
         q1(7)
         q2(7)
-        mm1_close(opened2, (4, 5, 6), (SC, VC))
-        mm1(7, (SC, VC))
+        mm1(3, (SC, SC))
+        for a in (4, 5, 6, 7):
+            mm1_late(a)
         for j in range(4):
-            mm0(3, j, (SC, VC))
+            mm0(3, j, (SC, SC))

from contextlib import ExitStack

import concourse.mybir as mybir
from concourse.masks import make_identity

T, D = 2048, 1024
FLOPS = 2 * 2 * T * D * D
BYTES = T * D * (2 + 4 + 2 + 4) + D * D * (2 + 4)

F32 = mybir.dt.float32
BF16 = mybir.dt.bfloat16
U32 = mybir.dt.uint32
U8 = mybir.dt.uint8
E4 = mybir.dt.float8_e4m3fn_x4
E5 = mybir.dt.float8_e5m2_x4
ACT = mybir.ActivationFunctionType
ALU = mybir.AluOpType

P = 128
NB = 8


def tile_gnn_layer_pb_v_kernel(
    tc, BB_feature, RF_feature, W_bbbb, b_bbbb, W_rfbb, b_rfbb, z, grad_out, out_0, out_1
):
    nc = tc.nc
    x_v = BB_feature.flatten_outer_dims().rearrange("(c p j) w -> p c j w", p=P, j=4)
    z_v = z.flatten_outer_dims().rearrange("(c p j) w -> p c j w", p=P, j=4)
    g_v = grad_out.flatten_outer_dims().rearrange("(c p j) w -> p c j w", p=P, j=4)
    o0_v = out_0.flatten_outer_dims().rearrange("(c p j) w -> p c j w", p=P, j=4)
    w_v = W_bbbb.rearrange("(c p j) w -> p c j w", p=P, j=4)

    with ExitStack() as ctx:
        keep = ctx.enter_context(tc.tile_pool(name="keep", bufs=1))
        work = ctx.enter_context(tc.tile_pool(name="work", bufs=2))
        psum = ctx.enter_context(tc.psum_pool(name="psum", bufs=2))

        ident = keep.tile([P, P], F32, name="ident")
        make_identity(nc, ident[:])
        identb = keep.tile([P, P], BF16, name="identb")
        make_identity(nc, identb[:])
        warm = keep.tile([P, 8], F32, name="warm")
        nc.vector.memset(warm[:], 0.0)

        w_codes = keep.tile([P, 2, D], U32, name="w_codes", align_bytes=64)
        w_scales = keep.tile([P, 2, D], U8, name="w_scales", align_bytes=64)
        x_codes = keep.tile([P, 4, D], U32, name="x_codes", align_bytes=64)
        x_scales = keep.tile([P, 4, D], U8, name="x_scales", align_bytes=64)
        d_codes = keep.tile([P, 4, D], U32, name="d_codes", align_bytes=64)
        d_scales = keep.tile([P, 4, D], U8, name="d_scales", align_bytes=64)

        ctx.enter_context(tc.manual_schedule())
        nc.scalar.activation(out=warm[:, 4:5], in_=warm[:, 0:1], func=ACT.Sigmoid)

        zt, st, ut, gt, dzp, dzg, gtr, tq, ts, raw = {}, {}, {}, {}, {}, {}, {}, {}, {}, {}

        def cols(h):
            return slice(512 * h, 512 * (h + 1))

        def load_z(k):
            zt[k] = work.tile([P, 2048], F32, name="zt", bufs=4)
            nc.sync.dma_start(out=zt[k][:].rearrange("p (j w) -> p j w", j=4), in_=z_v[:, k // 2, :, cols(k % 2)])

        def load_g(k):
            gt[k] = work.tile([P, 2048], BF16, name="gt", bufs=4)
            nc.sync.dma_start(out=gt[k][:].rearrange("p (j w) -> p j w", j=4), in_=g_v[:, k // 2, :, cols(k % 2)])

        def load_raw(key, src, split=False):
            raw[key] = work.tile([P, 4, D], BF16, name="raw", bufs=2)
            if split:
                for ih in range(2):
                    nc.sync.dma_start(out=raw[key][:, :, cols(ih)], in_=src[:, :, cols(ih)])
            else:
                nc.sync.dma_start(out=raw[key][:], in_=src)

        def s1(k):
            st[k] = work.tile([P, 2048], F32, name="st", bufs=4)
            nc.scalar.activation(out=st[k][:], in_=zt[k][:], func=ACT.Sigmoid)

        def s2(k):
            ut[k] = work.tile([P, 2048], F32, name="ut", bufs=4)
            nc.scalar.activation(out=ut[k][:], in_=st[k][:], func=ACT.Ln, bias=1.0, scale=-1.0)

        def s3(k):
            nc.scalar.activation(out=ut[k][:], in_=ut[k][:], func=ACT.Sigmoid, scale=-2.0)

        def v1(k):
            nc.vector.scalar_tensor_tensor(out=zt[k][:], in0=zt[k][:], scalar=-4.0, in1=st[k][:], op0=ALU.mult, op1=ALU.mult)

        def v2(k):
            nc.vector.scalar_tensor_tensor(out=st[k][:], in0=ut[k][:], scalar=1.0, in1=zt[k][:], op0=ALU.subtract, op1=ALU.mult)

        def v3(k):
            nc.vector.scalar_tensor_tensor(out=zt[k][:], in0=st[k][:], scalar=2.0, in1=ut[k][:], op0=ALU.add, op1=ALU.mult)

        def v4(k):
            dzp[k] = work.tile([P, 2048], BF16, name="dzp", bufs=2, align_bytes=64)
            nc.vector.scalar_tensor_tensor(out=dzp[k][:], in0=zt[k][:], scalar=1.0, in1=gt[k][:], op0=ALU.subtract, op1=ALU.mult)

        def interleave(copy, dst, src):
            copy(out=dst.rearrange("p (c i j) -> p c j i", i=4, j=4), in_=src.rearrange("p j (c i) -> p c j i", i=4))

        def il_direct(k, copy):
            dzg[k] = work.tile([P, 2048], BF16, name="dzg", bufs=2, align_bytes=64)
            interleave(copy, dzg[k][:], dzp[k][:].rearrange("p (j w) -> p j w", j=4))

        def il(k, copies):
            dzg[k] = work.tile([P, 2048], BF16, name="dzg", bufs=2, align_bytes=64)
            src = dzp[k][:].rearrange("p (j w) -> p w j", j=4)
            for half in range(2):
                ilp = psum.tile([P, 1024], BF16, name="ilp", tag="bank", bufs=8)
                for qd in range(2):
                    w0 = 256 * half + 128 * qd
                    nc.tensor.matmul(
                        out=ilp[:, 512 * qd : 512 * (qd + 1)].rearrange("p (w j) -> p w j", j=4),
                        lhsT=identb[:],
                        rhs=src[:, w0 : w0 + 128, :],
                        start=True,
                        stop=True,
                    )
                copies[half](out=dzg[k][:, 1024 * half : 1024 * (half + 1)], in_=ilp[:])

        def q1(k):
            nc.vector.quantize_mx(out=d_codes[:, k // 2, cols(k % 2)].bitcast(E5), scales=d_scales[:, k // 2, cols(k % 2)], in_=dzg[k][:])

        def tp(k, copies):
            gtr[k] = work.tile([P, 2048], BF16, name="gtr", bufs=2, align_bytes=64)
            words = dzp[k][:].bitcast(F32)
            dst = gtr[k][:].bitcast(F32).rearrange("p (j r u) -> p j r u", j=4, u=2)
            for half in range(2):
                xt = psum.tile([P, 4, P], F32, name="xt", tag="bank", bufs=8)
                for jj in range(2):
                    j = 2 * half + jj
                    for u in range(2):
                        nc.tensor.transpose(xt[:, 2 * jj + u, :], words[:, 256 * j + u : 256 * (j + 1) : 2], ident[:])
                copies[half](out=dst[:, 2 * half : 2 * half + 2], in_=xt[:].rearrange("p (j u) r -> p j r u", u=2))

        def q2(k):
            tq[k] = work.tile([P, 512], U32, name="tq", bufs=4, align_bytes=64)
            ts[k] = work.tile([P, 512], U8, name="ts", bufs=4, align_bytes=64)
            nc.vector.quantize_mx(out=tq[k][:].bitcast(E5), scales=ts[k][:], in_=gtr[k][:])

        grp = {}

        def prep_il(key, ih, copy):
            grp[(key, ih)] = work.tile([P, 2048], BF16, name="grp", bufs=2, align_bytes=64)
            interleave(copy, grp[(key, ih)][:], raw[key][:, :, cols(ih)])

        def prep_q(key, ih, codes, scales):
            nc.vector.quantize_mx(out=codes[:, cols(ih)].bitcast(E4), scales=scales[:, cols(ih)], in_=grp[(key, ih)][:])

        def mm0(c, j, copies):
            o_sb = work.tile([P, D], F32, name="o_sb", bufs=4)
            for ih in range(2):
                acc = psum.tile([P, 512], F32, name="acc", tag="bank", bufs=8)
                for h in range(2):
                    k = 2 * c + h
                    nc.tensor.matmul_mx(
                        out=acc[:],
                        lhsT=tq[k][:, P * j : P * (j + 1)].bitcast(E5),
                        lhsT_scale=ts[k][:, P * j : P * (j + 1)],
                        rhs=w_codes[:, h, cols(ih)].bitcast(E4),
                        rhs_scale=w_scales[:, h, cols(ih)],
                        start=(h == 0),
                        stop=(h == 1),
                    )
                copies[ih](out=o_sb[:, cols(ih)], in_=acc[:])
            nc.sync.dma_start(out=o0_v[:, c, j, :], in_=o_sb[:])

        def passes1(acc, a, ih, cs):
            for c in cs:
                nc.tensor.matmul_mx(
                    out=acc[:],
                    lhsT=d_codes[:, c, P * a : P * (a + 1)].bitcast(E5),
                    lhsT_scale=d_scales[:, c, P * a : P * (a + 1)],
                    rhs=x_codes[:, c, cols(ih)].bitcast(E4),
                    rhs_scale=x_scales[:, c, cols(ih)],
                    start=(c == cs[0]),
                    stop=(c == cs[-1]),
                )

        def mm1(a, copies):
            o_sb = work.tile([P, D], F32, name="o_sb", bufs=4)
            for ih in range(2):
                acc = psum.tile([P, 512], F32, name="acc", tag="bank", bufs=8)
                passes1(acc, a, ih, (0, 1, 2, 3))
                copies[ih](out=o_sb[:, cols(ih)], in_=acc[:])
            nc.sync.dma_start(out=out_1[P * a : P * (a + 1), :], in_=o_sb[:])

        part = {}

        eacc = {}

        def early_mm(a):
            for ih in range(2):
                eacc[(a, ih)] = psum.tile([P, 512], F32, name="acc", tag="bank", bufs=8)
                passes1(eacc[(a, ih)], a, ih, (0, 1, 2))

        def early_copy(a):
            if a % 2 == 0:
                part[a // 2] = work.tile([P, 2048], F32, name="st", bufs=4)
            for ih in range(2):
                lo = 1024 * (a % 2) + 512 * ih
                SC(out=part[a // 2][:, lo : lo + 512], in_=eacc[(a, ih)][:])

        def mm1_late(a):
            for ih in range(2):
                acc = psum.tile([P, 512], F32, name="acc", tag="bank", bufs=8)
                passes1(acc, a, ih, (3,))
                lo = 1024 * (a % 2) + 512 * ih
                nc.vector.tensor_tensor(out=part[a // 2][:, lo : lo + 512], in0=acc[:], in1=part[a // 2][:, lo : lo + 512], op=ALU.add)
            lo = 1024 * (a % 2)
            nc.sync.dma_start(out=out_1[P * a : P * (a + 1), :], in_=part[a // 2][:, lo : lo + 1024])

        VC = nc.vector.tensor_copy
        SC = nc.scalar.copy

        def prep(key, codes, scales):
            prep_il(key, 0, VC)
            prep_il(key, 1, VC)
            prep_q(key, 0, codes, scales)
            prep_q(key, 1, codes, scales)


        def mm1_open(a_list):
            accs = {}
            for a in a_list:
                for ih in range(2):
                    accs[(a, ih)] = psum.tile([P, 512], F32, name="acc", tag="bank", bufs=8)
                    for c in (0, 1, 2):
                        nc.tensor.matmul_mx(
                            out=accs[(a, ih)][:],
                            lhsT=d_codes[:, c, P * a : P * (a + 1)].bitcast(E5),
                            lhsT_scale=d_scales[:, c, P * a : P * (a + 1)],
                            rhs=x_codes[:, c, cols(ih)].bitcast(E4),
                            rhs_scale=x_scales[:, c, cols(ih)],
                            start=(c == 0),
                            stop=False,
                        )
            return accs

        def mm1_close(accs, a_list, copies):
            for a in a_list:
                o_sb = work.tile([P, D], F32, name="o_sb", bufs=4)
                for ih in range(2):
                    nc.tensor.matmul_mx(
                        out=accs[(a, ih)][:],
                        lhsT=d_codes[:, 3, P * a : P * (a + 1)].bitcast(E5),
                        lhsT_scale=d_scales[:, 3, P * a : P * (a + 1)],
                        rhs=x_codes[:, 3, cols(ih)].bitcast(E4),
                        rhs_scale=x_scales[:, 3, cols(ih)],
                        start=False,
                        stop=True,
                    )
                    copies[ih](out=o_sb[:, cols(ih)], in_=accs[(a, ih)][:])
                nc.sync.dma_start(out=out_1[P * a : P * (a + 1), :], in_=o_sb[:])
        O0 = {0: ((SC, SC), (SC, SC), (SC, SC), (SC, SC)), 1: ((SC, SC), (SC, SC), (SC, SC), (SC, SC)), 2: ((SC, SC), (SC, SC), (SC, SC), (SC, SC))}
        XC = {0: (x_codes[:, 0], x_scales[:, 0]), 1: (x_codes[:, 1], x_scales[:, 1]), 2: (x_codes[:, 2], x_scales[:, 2]), 3: (x_codes[:, 3], x_scales[:, 3])}
        load_z(0)
        load_raw("w0", w_v[:, 0])
        load_z(1)
        load_raw("w1", w_v[:, 1])
        load_g(0)
        load_g(1)
        s1(0)
        prep("w0", w_codes[:, 0], w_scales[:, 0])
        load_raw("x0", x_v[:, 0])
        load_z(2)
        load_z(3)
        s1(1)
        v1(0)
        s2(0)
        s2(1)
        prep("w1", w_codes[:, 1], w_scales[:, 1])
        load_raw("x1", x_v[:, 1])
        load_g(2)
        load_g(3)
        v1(1)
        prep("x0", XC[0][0], XC[0][1])
        load_raw("x2", x_v[:, 2])
        s3(0)
        s3(1)

        for c in range(3):
            a, b = 2 * c, 2 * c + 1
            v2(a)
            v2(b)
            v3(a)
            v3(b)
            v4(a)
            v4(b)
            s1(a + 2)
            s1(b + 2)
            s2(a + 2)
            s2(b + 2)
            if c < 2:
                load_z(a + 4)
                load_z(b + 4)
                load_g(a + 4)
                load_g(b + 4)
            il(a, (SC, SC))
            tp(a, (SC, SC))
            il_direct(b, VC)
            tp(b, (SC, SC))
            v1(a + 2)
            v1(b + 2)
            s3(a + 2)
            s3(b + 2)
            q1(a)
            q2(a)
            q1(b)
            q2(b)
            prep_il("x%d" % (c + 1), 0, VC)
            prep_il("x%d" % (c + 1), 1, VC)
            for j in range(4):
                mm0(c, j, O0[c][j])
            if c < 2:
                prep_q("x%d" % (c + 1), 0, XC[c + 1][0], XC[c + 1][1])
                prep_q("x%d" % (c + 1), 1, XC[c + 1][0], XC[c + 1][1])
            if c == 0:
                load_raw("x3", x_v[:, 3])
        v2(6)
        prep_q("x3", 0, XC[3][0], XC[3][1])
        v3(6)
        prep_q("x3", 1, XC[3][0], XC[3][1])
        v4(6)
        for a in (4, 5):
            early_mm(a)
            early_copy(a)
        for a in (6, 7):
            early_mm(a)
        il_direct(6, SC)
        tp(6, (SC, SC))
        for a in (6, 7):
            early_copy(a)
        opened = mm1_open((0, 1))
        v2(7)
        q1(6)
        v3(7)
        q2(6)
        v4(7)
        mm1_close(opened, (0, 1), (SC, SC))
        mm1(2, (SC, SC))
        il_direct(7, VC)
        tp(7, (SC, SC))
        q1(7)
        q2(7)
        mm1(3, (SC, SC))
        for a in (4, 5, 6, 7):
            mm1_late(a)
        for j in range(4):
            mm0(3, j, (SC, SC))
